import numpy as np
import ml_dtypes


def mxq(x, axis, fmt="e4m3"):
    dtype, down = {"e4m3": (ml_dtypes.float8_e4m3fn, 7), "e5m2": (ml_dtypes.float8_e5m2, 14)}[fmt]
    v = np.moveaxis(np.asarray(x, np.float32).astype(ml_dtypes.bfloat16).astype(np.float64), axis, -1)
    blocks = v.reshape(v.shape[:-1] + (-1, 32))
    amax = np.abs(blocks).max(-1, keepdims=True)
    byte = np.maximum(np.where(amax > 0, np.frexp(amax)[1] - 1 + 127, 0) - down, 1)
    scale = np.exp2(byte - 127.0)
    codes = (blocks / scale).astype(np.float32).astype(dtype).astype(np.float64)
    return np.moveaxis((codes * scale).reshape(v.shape), -1, axis)


WIDE = False


def mx_kscale(k):
    if not WIDE:
        return np.ones(k)
    levels = np.array([10, -10, 5, -5, 0])
    a = np.random.permutation(np.resize(levels, k // 512 * 4)).reshape(k // 512, 4)
    idx = np.arange(k)
    return np.exp2(a[idx // 512, idx % 128 // 32])


BF16 = ml_dtypes.bfloat16


def bf(x):
    return np.asarray(x, np.float32).astype(BF16)


def f64(x):
    return np.asarray(x).astype(np.float64)


B, S, E, P, H = 4, 2048, 1024, 128, 4
D = P // H


def rope(x):
    inv_freq = 1.0 / (10000.0 ** (f64(np.arange(0, D, 2)) / D))
    t = f64(np.arange(S))
    freqs = np.repeat(t[:, None] * inv_freq[None, :], 2, axis=-1)
    cos, sin = np.cos(freqs), np.sin(freqs)
    xp = x.reshape(*x.shape[:-1], D // 2, 2)
    rot = np.stack((-xp[..., 1], xp[..., 0]), axis=-1).reshape(x.shape)
    return x * cos + rot * sin


def setup_inputs():
    s = mx_kscale(E)
    return {"emb": bf(np.random.standard_normal((B, S, E)) * s),
            "W1": bf(np.random.standard_normal((P, E)) * 0.6 / np.sqrt(E) / s),
            "W2": bf(np.random.standard_normal((P, E)) * 0.6 / np.sqrt(E) / s),
            "W3": bf(np.random.standard_normal((P, E)) * 2.0 / np.sqrt(E) / s)}


def reference(emb, W1, W2, W3):
    xq = mxq(f64(emb), 2, "e4m3")
    q = (xq @ mxq(f64(W1), 1, "e4m3").T).reshape(B, H, S, D)
    k = (xq @ mxq(f64(W2), 1, "e4m3").T).reshape(B, H, S, D)
    v = (xq @ mxq(f64(W3), 1, "e4m3").T).reshape(B, H, S, D)
    return rope(q), rope(k), v

@@ -1,0 +1,213 @@
+from contextlib import ExitStack
+
+import concourse.mybir as mybir
+from concourse.masks import make_identity
+
+F32 = mybir.dt.float32
+BF16 = mybir.dt.bfloat16
+I32 = mybir.dt.int32
+U32 = mybir.dt.uint32
+U8 = mybir.dt.uint8
+FP8X4 = mybir.dt.float8_e4m3fn_x4
+ALU = mybir.AluOpType
+ACT = mybir.ActivationFunctionType
+
+P = 128
+E = 1024
+TOKENS = 8192
+FLOPS = 2 * TOKENS * E * 384
+PI = 3.141592653589793
+NFREQ = 16
+CHUNKS = 16
+BATCHES = 32
+
+
+def round_bits(x, bits):
+    k = 1.0
+    while x * k < 2.0 ** (bits - 1):
+        k = k * 2.0
+    return round(x * k) / k
+
+
+PHI = [10000.0 ** (-i / 16.0) / (2.0 * PI) for i in range(NFREQ)]
+PHI_HI = [round_bits(v, 12) for v in PHI]
+PHI_LO = [PHI[i] - PHI_HI[i] for i in range(NFREQ)]
+
+
+def tile_attention_pa_t_kernel(tc, emb, W1, W2, W3, out_0, out_1, out_2):
+    nc = tc.nc
+    emb_v = emb.rearrange("b (h p j) k -> (b h) p (j k)", h=4, p=P, j=4)
+    out_v = [o.rearrange("b h (a x) d -> (b h) a (x d)", x=16) for o in (out_0, out_1, out_2)]
+
+    with ExitStack() as ctx:
+        const = ctx.enter_context(tc.tile_pool(name="const", bufs=1))
+        xpool = ctx.enter_context(tc.tile_pool(name="xpool", bufs=8))
+        gpool = ctx.enter_context(tc.tile_pool(name="gpool", bufs=3))
+        mpool = ctx.enter_context(tc.tile_pool(name="mpool", bufs=3))
+        ypool = ctx.enter_context(tc.tile_pool(name="ypool", bufs=4))
+        ps_t = ctx.enter_context(tc.psum_pool(name="ps_t", bufs=4))
+        ps_qk = ctx.enter_context(tc.psum_pool(name="ps_qk", bufs=2))
+        ps_v = ctx.enter_context(tc.psum_pool(name="ps_v", bufs=2))
+
+        w_raw = const.tile([P, 3, E], BF16)
+        for w, wap in enumerate((W1, W2, W3)):
+            nc.sync.dma_start(out=w_raw[:, w, :], in_=wap)
+
+        ident = const.tile([P, P], F32)
+        make_identity(nc, ident[:])
+
+        s_i = const.tile([P, 16], I32)
+        nc.gpsimd.iota(s_i[:], pattern=[[1, 16]], base=0, channel_multiplier=16)
+        s_f = const.tile([P, 16], F32)
+        nc.vector.tensor_copy(out=s_f[:], in_=s_i[:])
+        th = const.tile([P, 16, NFREQ], F32)
+        tl = const.tile([P, 16, NFREQ], F32)
+        for i in range(NFREQ):
+            nc.vector.tensor_scalar_mul(out=th[:, :, i], in0=s_f[:], scalar1=PHI_HI[i])
+            nc.scalar.mul(out=tl[:, :, i], in_=s_f[:], mul=PHI_LO[i])
+        tq = const.tile([P, 256], F32)
+        th2 = th[:].rearrange("p m i -> p (m i)")
+        tl2 = tl[:].rearrange("p m i -> p (m i)")
+        nc.vector.scalar_tensor_tensor(out=tq[:], in0=th2, scalar=0.25, in1=tl2, op0=ALU.add, op1=ALU.add)
+        n_i = const.tile([P, 256], I32)
+        nc.vector.tensor_copy(out=n_i[:], in_=tq[:])
+        n_f = const.tile([P, 256], F32)
+        nc.vector.tensor_copy(out=n_f[:], in_=n_i[:])
+        fr = const.tile([P, 256], F32)
+        nc.vector.tensor_tensor(out=fr[:], in0=th2, in1=n_f[:], op=ALU.subtract)
+        fr2 = const.tile([P, 256], F32)
+        nc.vector.tensor_tensor(out=fr2[:], in0=fr[:], in1=tl2, op=ALU.add)
+        hs = const.tile([P, 256], F32)
+        nc.scalar.activation(out=hs[:], in_=fr2[:], func=ACT.Sin, scale=PI)
+        qs = const.tile([P, 256], F32)
+        nc.scalar.activation(out=qs[:], in_=fr2[:], func=ACT.Sin, scale=PI / 2.0)
+        hs2 = const.tile([P, 256], F32)
+        nc.scalar.square(out=hs2[:], in_=hs[:])
+        qs2 = const.tile([P, 256], F32)
+        nc.scalar.square(out=qs2[:], in_=qs[:])
+        cpf = const.tile([P, 256], F32)
+        nc.vector.tensor_scalar(out=cpf[:], in0=qs2[:], scalar1=-4.0, scalar2=2.0, op0=ALU.mult, op1=ALU.add)
+        ctab = const.tile([P, 4, P], F32)
+        stab = const.tile([P, 4, P], F32)
+        ctab_v = ctab[:].rearrange("p j (n two) -> p (j n) two", two=2)
+        stab_v = stab[:].rearrange("p j (n two) -> p (j n) two", two=2)
+        nc.vector.tensor_scalar(
+            out=ctab_v, in0=hs2[:].unsqueeze(2).to_broadcast([P, 256, 2]),
+            scalar1=-2.0, scalar2=1.0, op0=ALU.mult, op1=ALU.add,
+        )
+        nc.vector.tensor_tensor(out=stab_v[:, :, 1], in0=hs[:], in1=cpf[:], op=ALU.mult)
+        nc.vector.tensor_scalar_mul(out=stab_v[:, :, 0], in0=stab_v[:, :, 1], scalar1=-1.0)
+
+        w_grp = const.tile([P, 2, 384, 4], BF16, align_bytes=64)
+        w_grp32 = w_grp[:].bitcast(F32)
+        w_raw32 = w_raw[:].bitcast(F32)
+        w_codes = const.tile([P, 2, 384], U32, align_bytes=64)
+        w_scales = const.tile([P, 2, 384], U8, align_bytes=64)
+        for w in range(3):
+            tp = ps_t.tile([P, 4, P], F32, tag="tp")
+            for wb in range(4):
+                nc.tensor.transpose(out=tp[:, wb, :], in_=w_raw32[:, w, wb * P:(wb + 1) * P], identity=ident[:])
+            nc.scalar.copy(
+                out=w_grp32[:, :, w * P:(w + 1) * P, :],
+                in_=tp[:].rearrange("p (g u) r -> p g r u", u=2),
+            )
+        for g in range(2):
+            for lo, hi in ((0, 256), (256, 384)):
+                nc.vector.quantize_mx(
+                    out=w_codes[:, g, lo:hi].bitcast(FP8X4),
+                    scales=w_scales[:, g, lo:hi],
+                    in_=w_grp[:, g, lo:hi, :].rearrange("p f t -> p (f t)"),
+                )
+
+        state = {}
+
+        def stage_a(b):
+            n, bb = divmod(b, 2)
+            if bb == 0:
+                x = xpool.tile([P, 4, E], BF16, tag="x")
+                nc.sync.dma_start(out=x[:].rearrange("p j k -> p (j k)"), in_=emb_v[n])
+                state["x"] = x
+            x32 = state["x"][:].bitcast(F32)
+            grp = gpool.tile([P, 2, 2, P, 4], BF16, tag="grp", align_bytes=64)
+            grp32 = grp[:].bitcast(F32)
+            for jj in range(2):
+                tp = ps_t.tile([P, 4, P], F32, tag="tp")
+                for wb in range(4):
+                    nc.tensor.transpose(
+                        out=tp[:, wb, :], in_=x32[:, 2 * bb + jj, wb * P:(wb + 1) * P], identity=ident[:]
+                    )
+                nc.scalar.copy(out=grp32[:, jj], in_=tp[:].rearrange("p (g u) r -> p g r u", u=2))
+            state[("grp", b)] = grp
+
+        def stage_b(b):
+            grp = state[("grp", b)]
+            codes = gpool.tile([P, 512], U32, tag="codes", align_bytes=64)
+            scales = gpool.tile([P, 512], U8, tag="scales", align_bytes=64)
+            nc.vector.quantize_mx(
+                out=codes[:].bitcast(FP8X4), scales=scales[:],
+                in_=grp[:].rearrange("p a g r t -> p (a g r t)"),
+            )
+            state[("q", b)] = (codes, scales)
+
+        def stage_c(b):
+            codes, scales = state[("q", b)]
+            qk = ps_qk.tile([P, 2, 256], F32, tag="qk")
+            vb = ps_v.tile([P, 2, P], F32, tag="vb")
+            for jj in range(2):
+                for g in range(2):
+                    c0 = (jj * 2 + g) * P
+                    for dst, lo, hi in ((qk[:, jj, :], 0, 256), (vb[:, jj, :], 256, 384)):
+                        nc.tensor.matmul_mx(
+                            out=dst,
+                            lhsT=codes[:, c0:c0 + P].bitcast(FP8X4),
+                            lhsT_scale=scales[:, c0:c0 + P],
+                            rhs=w_codes[:, g, lo:hi].bitcast(FP8X4),
+                            rhs_scale=w_scales[:, g, lo:hi],
+                            start=(g == 0), stop=(g == 1),
+                        )
+            state[("ps", b)] = (qk, vb)
+
+        def stage_d(b):
+            n, bb = divmod(b, 2)
+            qk, vb = state[("ps", b)]
+            if bb == 0:
+                y = ypool.tile([P, 2, 4, P], F32, tag="y")
+                yv = ypool.tile([P, 4, P], F32, tag="yv")
+                state["y"] = (y, yv)
+            y, yv = state["y"]
+            shape5 = [P, 2, 2, 64, 2]
+            m1 = mpool.tile([P, 512], F32, tag="m1")
+            m2 = mpool.tile([P, 512], F32, tag="m2")
+            js = slice(2 * bb, 2 * bb + 2)
+            ct = ctab[:, js, :].rearrange("p a (n two) -> p a n two", two=2).unsqueeze(2).to_broadcast(shape5)
+            st = stab[:, js, :].rearrange("p a (n two) -> p a n two", two=2).unsqueeze(2).to_broadcast(shape5)
+            x5 = qk[:].rearrange("p a (q n two) -> p a q n two", q=2, two=2)
+            nc.vector.tensor_tensor(
+                out=m1[:].rearrange("p (a q n two) -> p a q n two", a=2, q=2, two=2), in0=x5, in1=ct, op=ALU.mult
+            )
+            nc.vector.tensor_tensor(
+                out=m2[:].rearrange("p (a q n two) -> p a q n two", a=2, q=2, two=2),
+                in0=x5[:, :, :, :, ::-1], in1=st, op=ALU.mult,
+            )
+            nc.gpsimd.tensor_tensor(
+                out=y[:, :, js, :].rearrange("p q a f -> p a q f"),
+                in0=m1[:].rearrange("p (a q f) -> p a q f", a=2, q=2),
+                in1=m2[:].rearrange("p (a q f) -> p a q f", a=2, q=2),
+                op=ALU.add,
+            )
+            nc.scalar.copy(out=yv[:, js, :], in_=vb[:])
+            if bb == 1:
+                nc.sync.dma_start(out=out_v[0][n], in_=y[:, 0].rearrange("p j f -> p (j f)"))
+                nc.sync.dma_start(out=out_v[1][n], in_=y[:, 1].rearrange("p j f -> p (j f)"))
+                nc.sync.dma_start(out=out_v[2][n], in_=yv[:].rearrange("p j f -> p (j f)"))
+
+        stage_a(0)
+        stage_a(1)
+        stage_b(0)
+        for b in range(BATCHES):
+            if b + 2 < BATCHES:
+                stage_a(b + 2)
+            if b + 1 < BATCHES:
+                stage_b(b + 1)
+            stage_c(b)
+            stage_d(b)

@@ -20,6 +20,9 @@ PI = 3.141592653589793
 NFREQ = 16
 CHUNKS = 16
 BATCHES = 32
+AHEAD = 10
+MANUAL = True
+DEP = False
 
 
 def round_bits(x, bits):
@@ -41,20 +44,35 @@ def tile_attention_pa_t_kernel(tc, emb, W1, W2, W3, out_0, out_1, out_2):
 
     with ExitStack() as ctx:
         const = ctx.enter_context(tc.tile_pool(name="const", bufs=1))
-        xpool = ctx.enter_context(tc.tile_pool(name="xpool", bufs=8))
+        xpool = ctx.enter_context(tc.tile_pool(name="xpool", bufs=AHEAD))
         gpool = ctx.enter_context(tc.tile_pool(name="gpool", bufs=3))
         mpool = ctx.enter_context(tc.tile_pool(name="mpool", bufs=3))
-        ypool = ctx.enter_context(tc.tile_pool(name="ypool", bufs=4))
+        ypool = ctx.enter_context(tc.tile_pool(name="ypool", bufs=6))
         ps_t = ctx.enter_context(tc.psum_pool(name="ps_t", bufs=4))
         ps_qk = ctx.enter_context(tc.psum_pool(name="ps_qk", bufs=2))
         ps_v = ctx.enter_context(tc.psum_pool(name="ps_v", bufs=2))
 
+        ident = const.tile([P, P], F32)
+        make_identity(nc, ident[:])
+        if MANUAL:
+            ctx.enter_context(tc.manual_schedule())
+
+        state = {}
+
+        def load(n):
+            x = xpool.tile([P, 4, E], BF16, tag="x")
+            if n == 0:
+                nc.sync.dma_start(out=x[:, 0:2, :].rearrange("p j k -> p (j k)"), in_=emb_v[n][:, 0:2 * E])
+                nc.sync.dma_start(out=x[:, 2:4, :].rearrange("p j k -> p (j k)"), in_=emb_v[n][:, 2 * E:4 * E])
+            else:
+                nc.sync.dma_start(out=x[:].rearrange("p j k -> p (j k)"), in_=emb_v[n])
+            state[("x", n)] = x
+
         w_raw = const.tile([P, 3, E], BF16)
         for w, wap in enumerate((W1, W2, W3)):
             nc.sync.dma_start(out=w_raw[:, w, :], in_=wap)
-
-        ident = const.tile([P, P], F32)
-        make_identity(nc, ident[:])
+        for n in range(AHEAD):
+            load(n)
 
         s_i = const.tile([P, 16], I32)
         nc.gpsimd.iota(s_i[:], pattern=[[1, 16]], base=0, channel_multiplier=16)
@@ -85,18 +103,6 @@ def tile_attention_pa_t_kernel(tc, emb, W1, W2, W3, out_0, out_1, out_2):
         nc.scalar.square(out=hs2[:], in_=hs[:])
         qs2 = const.tile([P, 256], F32)
         nc.scalar.square(out=qs2[:], in_=qs[:])
-        cpf = const.tile([P, 256], F32)
-        nc.vector.tensor_scalar(out=cpf[:], in0=qs2[:], scalar1=-4.0, scalar2=2.0, op0=ALU.mult, op1=ALU.add)
-        ctab = const.tile([P, 4, P], F32)
-        stab = const.tile([P, 4, P], F32)
-        ctab_v = ctab[:].rearrange("p j (n two) -> p (j n) two", two=2)
-        stab_v = stab[:].rearrange("p j (n two) -> p (j n) two", two=2)
-        nc.vector.tensor_scalar(
-            out=ctab_v, in0=hs2[:].unsqueeze(2).to_broadcast([P, 256, 2]),
-            scalar1=-2.0, scalar2=1.0, op0=ALU.mult, op1=ALU.add,
-        )
-        nc.vector.tensor_tensor(out=stab_v[:, :, 1], in0=hs[:], in1=cpf[:], op=ALU.mult)
-        nc.vector.tensor_scalar_mul(out=stab_v[:, :, 0], in0=stab_v[:, :, 1], scalar1=-1.0)
 
         w_grp = const.tile([P, 2, 384, 4], BF16, align_bytes=64)
         w_grp32 = w_grp[:].bitcast(F32)
@@ -119,15 +125,24 @@ def tile_attention_pa_t_kernel(tc, emb, W1, W2, W3, out_0, out_1, out_2):
                     in_=w_grp[:, g, lo:hi, :].rearrange("p f t -> p (f t)"),
                 )
 
-        state = {}
+        ctab = const.tile([P, 4, P], F32)
+        stab = const.tile([P, 4, P], F32)
+
+        def tables_part2():
+            cpf = const.tile([P, 256], F32)
+            nc.vector.tensor_scalar(out=cpf[:], in0=qs2[:], scalar1=-4.0, scalar2=2.0, op0=ALU.mult, op1=ALU.add)
+            ctab_v = ctab[:].rearrange("p j (n two) -> p (j n) two", two=2)
+            stab_v = stab[:].rearrange("p j (n two) -> p (j n) two", two=2)
+            nc.vector.tensor_scalar(
+                out=ctab_v, in0=hs2[:].unsqueeze(2).to_broadcast([P, 256, 2]),
+                scalar1=-2.0, scalar2=1.0, op0=ALU.mult, op1=ALU.add,
+            )
+            nc.vector.tensor_tensor(out=stab_v[:, :, 1], in0=hs[:], in1=cpf[:], op=ALU.mult)
+            nc.vector.tensor_scalar_mul(out=stab_v[:, :, 0], in0=stab_v[:, :, 1], scalar1=-1.0)
 
         def stage_a(b):
             n, bb = divmod(b, 2)
-            if bb == 0:
-                x = xpool.tile([P, 4, E], BF16, tag="x")
-                nc.sync.dma_start(out=x[:].rearrange("p j k -> p (j k)"), in_=emb_v[n])
-                state["x"] = x
-            x32 = state["x"][:].bitcast(F32)
+            x32 = state[("x", n)][:].bitcast(F32)
             grp = gpool.tile([P, 2, 2, P, 4], BF16, tag="grp", align_bytes=64)
             grp32 = grp[:].bitcast(F32)
             for jj in range(2):
@@ -148,6 +163,9 @@ def tile_attention_pa_t_kernel(tc, emb, W1, W2, W3, out_0, out_1, out_2):
                 in_=grp[:].rearrange("p a g r t -> p (a g r t)"),
             )
             state[("q", b)] = (codes, scales)
+            if DEP:
+                junk = mpool.tile([P, 1], F32, tag="junk")
+                nc.gpsimd.tensor_copy(out=junk[:], in_=codes[:, 0:1].bitcast(F32))
 
         def stage_c(b):
             codes, scales = state[("q", b)]
@@ -167,14 +185,18 @@ def tile_attention_pa_t_kernel(tc, emb, W1, W2, W3, out_0, out_1, out_2):
                         )
             state[("ps", b)] = (qk, vb)
 
-        def stage_d(b):
+        def stage_v(b):
             n, bb = divmod(b, 2)
             qk, vb = state[("ps", b)]
             if bb == 0:
-                y = ypool.tile([P, 2, 4, P], F32, tag="y")
                 yv = ypool.tile([P, 4, P], F32, tag="yv")
-                state["y"] = (y, yv)
-            y, yv = state["y"]
+                state[("yv", n)] = yv
+            yv = state[("yv", n)]
+            nc.scalar.copy(out=yv[:, 2 * bb:2 * bb + 2, :], in_=vb[:])
+
+        def stage_m(b):
+            n, bb = divmod(b, 2)
+            qk, vb = state[("ps", b)]
             shape5 = [P, 2, 2, 64, 2]
             m1 = mpool.tile([P, 512], F32, tag="m1")
             m2 = mpool.tile([P, 512], F32, tag="m2")
@@ -189,25 +211,43 @@ def tile_attention_pa_t_kernel(tc, emb, W1, W2, W3, out_0, out_1, out_2):
                 out=m2[:].rearrange("p (a q n two) -> p a q n two", a=2, q=2, two=2),
                 in0=x5[:, :, :, :, ::-1], in1=st, op=ALU.mult,
             )
+            state[("m", b)] = (m1, m2)
+
+        def stage_add(b):
+            n, bb = divmod(b, 2)
+            m1, m2 = state[("m", b)]
+            if bb == 0:
+                y = ypool.tile([P, 2, 4, P], F32, tag="y")
+                state[("y", n)] = y
+            y = state[("y", n)]
+            js = slice(2 * bb, 2 * bb + 2)
             nc.gpsimd.tensor_tensor(
                 out=y[:, :, js, :].rearrange("p q a f -> p a q f"),
                 in0=m1[:].rearrange("p (a q f) -> p a q f", a=2, q=2),
                 in1=m2[:].rearrange("p (a q f) -> p a q f", a=2, q=2),
                 op=ALU.add,
             )
-            nc.scalar.copy(out=yv[:, js, :], in_=vb[:])
             if bb == 1:
+                yv = state[("yv", n)]
                 nc.sync.dma_start(out=out_v[0][n], in_=y[:, 0].rearrange("p j f -> p (j f)"))
                 nc.sync.dma_start(out=out_v[1][n], in_=y[:, 1].rearrange("p j f -> p (j f)"))
                 nc.sync.dma_start(out=out_v[2][n], in_=yv[:].rearrange("p j f -> p (j f)"))
+                if n + AHEAD < CHUNKS:
+                    load(n + AHEAD)
 
         stage_a(0)
         stage_a(1)
         stage_b(0)
-        for b in range(BATCHES):
+        tables_part2()
+        for b in range(BATCHES + 1):
+            if b < BATCHES:
+                stage_c(b)
+                stage_v(b)
             if b + 2 < BATCHES:
                 stage_a(b + 2)
             if b + 1 < BATCHES:
                 stage_b(b + 1)
-            stage_c(b)
-            stage_d(b)
+            if b >= 1:
+                stage_add(b - 1)
+            if b < BATCHES:
+                stage_m(b)

@@ -21,8 +21,6 @@ NFREQ = 16
 CHUNKS = 16
 BATCHES = 32
 AHEAD = 10
-MANUAL = True
-DEP = False
 
 
 def round_bits(x, bits):
@@ -45,37 +43,50 @@ def tile_attention_pa_t_kernel(tc, emb, W1, W2, W3, out_0, out_1, out_2):
     with ExitStack() as ctx:
         const = ctx.enter_context(tc.tile_pool(name="const", bufs=1))
         xpool = ctx.enter_context(tc.tile_pool(name="xpool", bufs=AHEAD))
-        gpool = ctx.enter_context(tc.tile_pool(name="gpool", bufs=3))
-        mpool = ctx.enter_context(tc.tile_pool(name="mpool", bufs=3))
+        gpool = ctx.enter_context(tc.tile_pool(name="gpool", bufs=4))
+        kpool = ctx.enter_context(tc.tile_pool(name="kpool", bufs=5))
+        mpool = ctx.enter_context(tc.tile_pool(name="mpool", bufs=4))
         ypool = ctx.enter_context(tc.tile_pool(name="ypool", bufs=6))
         ps_t = ctx.enter_context(tc.psum_pool(name="ps_t", bufs=4))
         ps_qk = ctx.enter_context(tc.psum_pool(name="ps_qk", bufs=2))
         ps_v = ctx.enter_context(tc.psum_pool(name="ps_v", bufs=2))
 
+        s_i = const.tile([P, 16], I32)
+        nc.gpsimd.iota(s_i[:], pattern=[[1, 16]], base=0, channel_multiplier=16)
         ident = const.tile([P, P], F32)
         make_identity(nc, ident[:])
-        if MANUAL:
-            ctx.enter_context(tc.manual_schedule())
+        ctx.enter_context(tc.manual_schedule())
 
         state = {}
 
         def load(n):
             x = xpool.tile([P, 4, E], BF16, tag="x")
-            if n == 0:
-                nc.sync.dma_start(out=x[:, 0:2, :].rearrange("p j k -> p (j k)"), in_=emb_v[n][:, 0:2 * E])
-                nc.sync.dma_start(out=x[:, 2:4, :].rearrange("p j k -> p (j k)"), in_=emb_v[n][:, 2 * E:4 * E])
-            else:
-                nc.sync.dma_start(out=x[:].rearrange("p j k -> p (j k)"), in_=emb_v[n])
             state[("x", n)] = x
+            if n > 0:
+                nc.sync.dma_start(out=x[:].rearrange("p j k -> p (j k)"), in_=emb_v[n])
+
+        def load_half(bb):
+            x = state[("x", 0)]
+            nc.sync.dma_start(
+                out=x[:, 2 * bb:2 * bb + 2, :].rearrange("p j k -> p (j k)"),
+                in_=emb_v[0][:, 2 * bb * E:(2 * bb + 2) * E],
+            )
 
         w_raw = const.tile([P, 3, E], BF16)
-        for w, wap in enumerate((W1, W2, W3)):
-            nc.sync.dma_start(out=w_raw[:, w, :], in_=wap)
-        for n in range(AHEAD):
+        w_aps = (W1, W2, W3)
+        load(0)
+        nc.sync.dma_start(out=w_raw[:, 0, :], in_=w_aps[0])
+        nc.sync.dma_start(out=w_raw[:, 1, :], in_=w_aps[1])
+        load_half(0)
+        nc.sync.dma_start(out=w_raw[:, 2, :], in_=w_aps[2])
+        load_half(1)
+        for n in range(1, AHEAD):
             load(n)
 
-        s_i = const.tile([P, 16], I32)
-        nc.gpsimd.iota(s_i[:], pattern=[[1, 16]], base=0, channel_multiplier=16)
+        zero = const.tile([P, 1], F32)
+        nc.vector.memset(zero[:], 0.0)
+        warm = const.tile([P, 1], F32)
+        nc.scalar.activation(out=warm[:], in_=zero[:], func=ACT.Sin, scale=1.0)
         s_f = const.tile([P, 16], F32)
         nc.vector.tensor_copy(out=s_f[:], in_=s_i[:])
         th = const.tile([P, 16, NFREQ], F32)
@@ -89,46 +100,25 @@ def tile_attention_pa_t_kernel(tc, emb, W1, W2, W3, out_0, out_1, out_2):
         nc.vector.scalar_tensor_tensor(out=tq[:], in0=th2, scalar=0.25, in1=tl2, op0=ALU.add, op1=ALU.add)
         n_i = const.tile([P, 256], I32)
         nc.vector.tensor_copy(out=n_i[:], in_=tq[:])
-        n_f = const.tile([P, 256], F32)
-        nc.vector.tensor_copy(out=n_f[:], in_=n_i[:])
         fr = const.tile([P, 256], F32)
-        nc.vector.tensor_tensor(out=fr[:], in0=th2, in1=n_f[:], op=ALU.subtract)
+        nc.vector.tensor_tensor(out=fr[:], in0=th2, in1=n_i[:], op=ALU.subtract)
         fr2 = const.tile([P, 256], F32)
         nc.vector.tensor_tensor(out=fr2[:], in0=fr[:], in1=tl2, op=ALU.add)
         hs = const.tile([P, 256], F32)
-        nc.scalar.activation(out=hs[:], in_=fr2[:], func=ACT.Sin, scale=PI)
         qs = const.tile([P, 256], F32)
-        nc.scalar.activation(out=qs[:], in_=fr2[:], func=ACT.Sin, scale=PI / 2.0)
         hs2 = const.tile([P, 256], F32)
-        nc.scalar.square(out=hs2[:], in_=hs[:])
         qs2 = const.tile([P, 256], F32)
-        nc.scalar.square(out=qs2[:], in_=qs[:])
 
-        w_grp = const.tile([P, 2, 384, 4], BF16, align_bytes=64)
-        w_grp32 = w_grp[:].bitcast(F32)
-        w_raw32 = w_raw[:].bitcast(F32)
-        w_codes = const.tile([P, 2, 384], U32, align_bytes=64)
-        w_scales = const.tile([P, 2, 384], U8, align_bytes=64)
-        for w in range(3):
-            tp = ps_t.tile([P, 4, P], F32, tag="tp")
-            for wb in range(4):
-                nc.tensor.transpose(out=tp[:, wb, :], in_=w_raw32[:, w, wb * P:(wb + 1) * P], identity=ident[:])
-            nc.scalar.copy(
-                out=w_grp32[:, :, w * P:(w + 1) * P, :],
-                in_=tp[:].rearrange("p (g u) r -> p g r u", u=2),
-            )
-        for g in range(2):
-            for lo, hi in ((0, 256), (256, 384)):
-                nc.vector.quantize_mx(
-                    out=w_codes[:, g, lo:hi].bitcast(FP8X4),
-                    scales=w_scales[:, g, lo:hi],
-                    in_=w_grp[:, g, lo:hi, :].rearrange("p f t -> p (f t)"),
-                )
+        def tables_scalar():
+            nc.scalar.activation(out=hs[:], in_=fr2[:], func=ACT.Sin, scale=PI)
+            nc.scalar.activation(out=qs[:], in_=fr2[:], func=ACT.Sin, scale=PI / 2.0)
+            nc.scalar.square(out=hs2[:], in_=hs[:])
+            nc.scalar.square(out=qs2[:], in_=qs[:])
 
         ctab = const.tile([P, 4, P], F32)
         stab = const.tile([P, 4, P], F32)
 
-        def tables_part2():
+        def tables_vector():
             cpf = const.tile([P, 256], F32)
             nc.vector.tensor_scalar(out=cpf[:], in0=qs2[:], scalar1=-4.0, scalar2=2.0, op0=ALU.mult, op1=ALU.add)
             ctab_v = ctab[:].rearrange("p j (n two) -> p (j n) two", two=2)
@@ -140,7 +130,33 @@ def tile_attention_pa_t_kernel(tc, emb, W1, W2, W3, out_0, out_1, out_2):
             nc.vector.tensor_tensor(out=stab_v[:, :, 1], in0=hs[:], in1=cpf[:], op=ALU.mult)
             nc.vector.tensor_scalar_mul(out=stab_v[:, :, 0], in0=stab_v[:, :, 1], scalar1=-1.0)
 
-        def stage_a(b):
+        w_grp = const.tile([P, 2, 384, 4], BF16, align_bytes=64)
+        w_grp32 = w_grp[:].bitcast(F32)
+        w_raw32 = w_raw[:].bitcast(F32)
+        w_codes = const.tile([P, 2, 384], U32, align_bytes=64)
+        w_scales = const.tile([P, 2, 384], U8, align_bytes=64)
+
+        def w_transpose(w):
+            tp = ps_t.tile([P, 4, P], F32, tag="tp")
+            for wb in range(4):
+                nc.tensor.transpose(out=tp[:, wb, :], in_=w_raw32[:, w, wb * P:(wb + 1) * P], identity=ident[:])
+            state[("wtp", w)] = tp
+
+        def w_copy(w):
+            nc.vector.tensor_copy(
+                out=w_grp32[:, :, w * P:(w + 1) * P, :],
+                in_=state[("wtp", w)][:].rearrange("p (g u) r -> p g r u", u=2),
+            )
+
+        def w_quantise(lo, hi):
+            for g in range(2):
+                nc.vector.quantize_mx(
+                    out=w_codes[:, g, lo:hi].bitcast(FP8X4),
+                    scales=w_scales[:, g, lo:hi],
+                    in_=w_grp[:, g, lo:hi, :].rearrange("p f t -> p (f t)"),
+                )
+
+        def transposes(b):
             n, bb = divmod(b, 2)
             x32 = state[("x", n)][:].bitcast(F32)
             grp = gpool.tile([P, 2, 2, P, 4], BF16, tag="grp", align_bytes=64)
@@ -154,20 +170,18 @@ def tile_attention_pa_t_kernel(tc, emb, W1, W2, W3, out_0, out_1, out_2):
                 nc.scalar.copy(out=grp32[:, jj], in_=tp[:].rearrange("p (g u) r -> p g r u", u=2))
             state[("grp", b)] = grp
 
-        def stage_b(b):
+        def quantise(b):
             grp = state[("grp", b)]
-            codes = gpool.tile([P, 512], U32, tag="codes", align_bytes=64)
-            scales = gpool.tile([P, 512], U8, tag="scales", align_bytes=64)
+            codes = kpool.tile([P, 512], U32, tag="codes", align_bytes=64)
+            scales = kpool.tile([P, 512], U8, tag="scales", align_bytes=64)
             nc.vector.quantize_mx(
                 out=codes[:].bitcast(FP8X4), scales=scales[:],
                 in_=grp[:].rearrange("p a g r t -> p (a g r t)"),
             )
             state[("q", b)] = (codes, scales)
-            if DEP:
-                junk = mpool.tile([P, 1], F32, tag="junk")
-                nc.gpsimd.tensor_copy(out=junk[:], in_=codes[:, 0:1].bitcast(F32))
 
-        def stage_c(b):
+        def products(b):
+            n, bb = divmod(b, 2)
             codes, scales = state[("q", b)]
             qk = ps_qk.tile([P, 2, 256], F32, tag="qk")
             vb = ps_v.tile([P, 2, P], F32, tag="vb")
@@ -183,20 +197,15 @@ def tile_attention_pa_t_kernel(tc, emb, W1, W2, W3, out_0, out_1, out_2):
                             rhs_scale=w_scales[:, g, lo:hi],
                             start=(g == 0), stop=(g == 1),
                         )
-            state[("ps", b)] = (qk, vb)
-
-        def stage_v(b):
-            n, bb = divmod(b, 2)
-            qk, vb = state[("ps", b)]
+            state[("qk", b)] = qk
             if bb == 0:
                 yv = ypool.tile([P, 4, P], F32, tag="yv")
                 state[("yv", n)] = yv
-            yv = state[("yv", n)]
-            nc.scalar.copy(out=yv[:, 2 * bb:2 * bb + 2, :], in_=vb[:])
+            nc.scalar.copy(out=state[("yv", n)][:, 2 * bb:2 * bb + 2, :], in_=vb[:])
 
-        def stage_m(b):
+        def rotate(b):
             n, bb = divmod(b, 2)
-            qk, vb = state[("ps", b)]
+            qk = state[("qk", b)]
             shape5 = [P, 2, 2, 64, 2]
             m1 = mpool.tile([P, 512], F32, tag="m1")
             m2 = mpool.tile([P, 512], F32, tag="m2")
@@ -213,41 +222,62 @@ def tile_attention_pa_t_kernel(tc, emb, W1, W2, W3, out_0, out_1, out_2):
             )
             state[("m", b)] = (m1, m2)
 
-        def stage_add(b):
+        def finish(b):
             n, bb = divmod(b, 2)
             m1, m2 = state[("m", b)]
             if bb == 0:
                 y = ypool.tile([P, 2, 4, P], F32, tag="y")
                 state[("y", n)] = y
             y = state[("y", n)]
+            yv = state[("yv", n)]
             js = slice(2 * bb, 2 * bb + 2)
-            nc.gpsimd.tensor_tensor(
+            eng = nc.vector if b == BATCHES - 1 else nc.gpsimd
+            eng.tensor_tensor(
                 out=y[:, :, js, :].rearrange("p q a f -> p a q f"),
                 in0=m1[:].rearrange("p (a q f) -> p a q f", a=2, q=2),
                 in1=m2[:].rearrange("p (a q f) -> p a q f", a=2, q=2),
                 op=ALU.add,
             )
-            if bb == 1:
-                yv = state[("yv", n)]
+            if n == CHUNKS - 1:
+                cs = slice(256 * bb, 256 * bb + 256)
+                nc.sync.dma_start(out=out_v[0][n][:, cs], in_=y[:, 0, js, :].rearrange("p j f -> p (j f)"))
+                nc.sync.dma_start(out=out_v[1][n][:, cs], in_=y[:, 1, js, :].rearrange("p j f -> p (j f)"))
+                nc.sync.dma_start(out=out_v[2][n][:, cs], in_=yv[:, js, :].rearrange("p j f -> p (j f)"))
+            elif bb == 1:
                 nc.sync.dma_start(out=out_v[0][n], in_=y[:, 0].rearrange("p j f -> p (j f)"))
                 nc.sync.dma_start(out=out_v[1][n], in_=y[:, 1].rearrange("p j f -> p (j f)"))
                 nc.sync.dma_start(out=out_v[2][n], in_=yv[:].rearrange("p j f -> p (j f)"))
                 if n + AHEAD < CHUNKS:
                     load(n + AHEAD)
 
-        stage_a(0)
-        stage_a(1)
-        stage_b(0)
-        tables_part2()
-        for b in range(BATCHES + 1):
-            if b < BATCHES:
-                stage_c(b)
-                stage_v(b)
-            if b + 2 < BATCHES:
-                stage_a(b + 2)
-            if b + 1 < BATCHES:
-                stage_b(b + 1)
-            if b >= 1:
-                stage_add(b - 1)
-            if b < BATCHES:
-                stage_m(b)
+        w_transpose(0)
+        w_transpose(1)
+        w_copy(0)
+        w_copy(1)
+        tables_scalar()
+        transposes(0)
+        w_quantise(0, 256)
+        w_transpose(2)
+        w_copy(2)
+        w_quantise(256, 384)
+        quantise(0)
+        transposes(1)
+        tables_vector()
+        quantise(1)
+        t_done = 1
+        q_done = 1
+        for k in range(-1, BATCHES):
+            t_up = min(BATCHES - 1, k + 4, 3 + (3 * k) // 2)
+            q_up = min(BATCHES - 1, k + 3, 2 + (3 * k) // 2) if k >= 0 else 1
+            while t_done < t_up:
+                t_done += 1
+                transposes(t_done)
+            if k + 1 < BATCHES:
+                products(k + 1)
+            if k >= 0:
+                rotate(k)
+            while q_done < q_up:
+                q_done += 1
+                quantise(q_done)
+            if k >= 0:
+                finish(k)

@@ -202,6 +202,8 @@ def tile_attention_pa_t_kernel(tc, emb, W1, W2, W3, out_0, out_1, out_2):
                 yv = ypool.tile([P, 4, P], F32, tag="yv")
                 state[("yv", n)] = yv
             nc.scalar.copy(out=state[("yv", n)][:, 2 * bb:2 * bb + 2, :], in_=vb[:])
+            if bb == 1:
+                nc.sync.dma_start(out=out_v[2][n], in_=state[("yv", n)][:].rearrange("p j f -> p (j f)"))
 
         def rotate(b):
             n, bb = divmod(b, 2)
@@ -229,24 +231,22 @@ def tile_attention_pa_t_kernel(tc, emb, W1, W2, W3, out_0, out_1, out_2):
                 y = ypool.tile([P, 2, 4, P], F32, tag="y")
                 state[("y", n)] = y
             y = state[("y", n)]
-            yv = state[("yv", n)]
             js = slice(2 * bb, 2 * bb + 2)
-            eng = nc.vector if b == BATCHES - 1 else nc.gpsimd
-            eng.tensor_tensor(
-                out=y[:, :, js, :].rearrange("p q a f -> p a q f"),
-                in0=m1[:].rearrange("p (a q f) -> p a q f", a=2, q=2),
-                in1=m2[:].rearrange("p (a q f) -> p a q f", a=2, q=2),
-                op=ALU.add,
-            )
+            m1v = m1[:].rearrange("p (a q f) -> p a q f", a=2, q=2)
+            m2v = m2[:].rearrange("p (a q f) -> p a q f", a=2, q=2)
+            cs = slice(256 * bb, 256 * bb + 256)
+            if b == BATCHES - 1:
+                for q in range(2):
+                    nc.vector.tensor_tensor(out=y[:, q, js, :], in0=m1v[:, :, q, :], in1=m2v[:, :, q, :], op=ALU.add)
+                    nc.sync.dma_start(out=out_v[q][n][:, cs], in_=y[:, q, js, :].rearrange("p j f -> p (j f)"))
+                return
+            nc.gpsimd.tensor_tensor(out=y[:, :, js, :].rearrange("p q a f -> p a q f"), in0=m1v, in1=m2v, op=ALU.add)
             if n == CHUNKS - 1:
-                cs = slice(256 * bb, 256 * bb + 256)
-                nc.sync.dma_start(out=out_v[0][n][:, cs], in_=y[:, 0, js, :].rearrange("p j f -> p (j f)"))
-                nc.sync.dma_start(out=out_v[1][n][:, cs], in_=y[:, 1, js, :].rearrange("p j f -> p (j f)"))
-                nc.sync.dma_start(out=out_v[2][n][:, cs], in_=yv[:, js, :].rearrange("p j f -> p (j f)"))
+                for q in range(2):
+                    nc.sync.dma_start(out=out_v[q][n][:, cs], in_=y[:, q, js, :].rearrange("p j f -> p (j f)"))
             elif bb == 1:
-                nc.sync.dma_start(out=out_v[0][n], in_=y[:, 0].rearrange("p j f -> p (j f)"))
-                nc.sync.dma_start(out=out_v[1][n], in_=y[:, 1].rearrange("p j f -> p (j f)"))
-                nc.sync.dma_start(out=out_v[2][n], in_=yv[:].rearrange("p j f -> p (j f)"))
+                for q in range(2):
+                    nc.sync.dma_start(out=out_v[q][n], in_=y[:, q].rearrange("p j f -> p (j f)"))
                 if n + AHEAD < CHUNKS:
                     load(n + AHEAD)
 
@@ -266,18 +266,18 @@ def tile_attention_pa_t_kernel(tc, emb, W1, W2, W3, out_0, out_1, out_2):
         quantise(1)
         t_done = 1
         q_done = 1
-        for k in range(-1, BATCHES):
-            t_up = min(BATCHES - 1, k + 4, 3 + (3 * k) // 2)
-            q_up = min(BATCHES - 1, k + 3, 2 + (3 * k) // 2) if k >= 0 else 1
+        for k in range(-2, BATCHES, 2):
+            for b in (k, k + 1):
+                if b >= 0:
+                    products(b)
+            t_up = min(BATCHES - 1, k + 5) if k >= 0 else 3
             while t_done < t_up:
                 t_done += 1
                 transposes(t_done)
-            if k + 1 < BATCHES:
-                products(k + 1)
-            if k >= 0:
-                rotate(k)
-            while q_done < q_up:
-                q_done += 1
-                quantise(q_done)
-            if k >= 0:
-                finish(k)
+            for b in (k, k + 1):
+                if b >= 0:
+                    rotate(b)
+                    while q_done < min(BATCHES - 1, b + 3):
+                        q_done += 1
+                        quantise(q_done)
+                    finish(b)

@@ -55,7 +55,6 @@ def tile_attention_pa_t_kernel(tc, emb, W1, W2, W3, out_0, out_1, out_2):
         nc.gpsimd.iota(s_i[:], pattern=[[1, 16]], base=0, channel_multiplier=16)
         ident = const.tile([P, P], F32)
         make_identity(nc, ident[:])
-        ctx.enter_context(tc.manual_schedule())
 
         state = {}
 

from contextlib import ExitStack

import concourse.mybir as mybir
from concourse.masks import make_identity

F32 = mybir.dt.float32
BF16 = mybir.dt.bfloat16
I32 = mybir.dt.int32
U32 = mybir.dt.uint32
U8 = mybir.dt.uint8
FP8X4 = mybir.dt.float8_e4m3fn_x4
ALU = mybir.AluOpType
ACT = mybir.ActivationFunctionType

P = 128
E = 1024
TOKENS = 8192
FLOPS = 2 * TOKENS * E * 384
PI = 3.141592653589793
NFREQ = 16
CHUNKS = 16
BATCHES = 32
AHEAD = 10


def round_bits(x, bits):
    k = 1.0
    while x * k < 2.0 ** (bits - 1):
        k = k * 2.0
    return round(x * k) / k


PHI = [10000.0 ** (-i / 16.0) / (2.0 * PI) for i in range(NFREQ)]
PHI_HI = [round_bits(v, 12) for v in PHI]
PHI_LO = [PHI[i] - PHI_HI[i] for i in range(NFREQ)]


def tile_attention_pa_t_kernel(tc, emb, W1, W2, W3, out_0, out_1, out_2):
    nc = tc.nc
    emb_v = emb.rearrange("b (h p j) k -> (b h) p (j k)", h=4, p=P, j=4)
    out_v = [o.rearrange("b h (a x) d -> (b h) a (x d)", x=16) for o in (out_0, out_1, out_2)]

    with ExitStack() as ctx:
        const = ctx.enter_context(tc.tile_pool(name="const", bufs=1))
        xpool = ctx.enter_context(tc.tile_pool(name="xpool", bufs=AHEAD))
        gpool = ctx.enter_context(tc.tile_pool(name="gpool", bufs=4))
        kpool = ctx.enter_context(tc.tile_pool(name="kpool", bufs=5))
        mpool = ctx.enter_context(tc.tile_pool(name="mpool", bufs=4))
        ypool = ctx.enter_context(tc.tile_pool(name="ypool", bufs=6))
        ps_t = ctx.enter_context(tc.psum_pool(name="ps_t", bufs=4))
        ps_qk = ctx.enter_context(tc.psum_pool(name="ps_qk", bufs=2))
        ps_v = ctx.enter_context(tc.psum_pool(name="ps_v", bufs=2))

        s_i = const.tile([P, 16], I32)
        nc.gpsimd.iota(s_i[:], pattern=[[1, 16]], base=0, channel_multiplier=16)
        ident = const.tile([P, P], F32)
        make_identity(nc, ident[:])

        state = {}

        def load(n):
            x = xpool.tile([P, 4, E], BF16, tag="x")
            state[("x", n)] = x
            if n > 0:
                nc.sync.dma_start(out=x[:].rearrange("p j k -> p (j k)"), in_=emb_v[n])

        def load_half(bb):
            x = state[("x", 0)]
            nc.sync.dma_start(
                out=x[:, 2 * bb:2 * bb + 2, :].rearrange("p j k -> p (j k)"),
                in_=emb_v[0][:, 2 * bb * E:(2 * bb + 2) * E],
            )

        w_raw = const.tile([P, 3, E], BF16)
        w_aps = (W1, W2, W3)
        load(0)
        nc.sync.dma_start(out=w_raw[:, 0, :], in_=w_aps[0])
        nc.sync.dma_start(out=w_raw[:, 1, :], in_=w_aps[1])
        load_half(0)
        nc.sync.dma_start(out=w_raw[:, 2, :], in_=w_aps[2])
        load_half(1)
        for n in range(1, AHEAD):
            load(n)

        zero = const.tile([P, 1], F32)
        nc.vector.memset(zero[:], 0.0)
        warm = const.tile([P, 1], F32)
        nc.scalar.activation(out=warm[:], in_=zero[:], func=ACT.Sin, scale=1.0)
        s_f = const.tile([P, 16], F32)
        nc.vector.tensor_copy(out=s_f[:], in_=s_i[:])
        th = const.tile([P, 16, NFREQ], F32)
        tl = const.tile([P, 16, NFREQ], F32)
        for i in range(NFREQ):
            nc.vector.tensor_scalar_mul(out=th[:, :, i], in0=s_f[:], scalar1=PHI_HI[i])
            nc.scalar.mul(out=tl[:, :, i], in_=s_f[:], mul=PHI_LO[i])
        tq = const.tile([P, 256], F32)
        th2 = th[:].rearrange("p m i -> p (m i)")
        tl2 = tl[:].rearrange("p m i -> p (m i)")
        nc.vector.scalar_tensor_tensor(out=tq[:], in0=th2, scalar=0.25, in1=tl2, op0=ALU.add, op1=ALU.add)
        n_i = const.tile([P, 256], I32)
        nc.vector.tensor_copy(out=n_i[:], in_=tq[:])
        fr = const.tile([P, 256], F32)
        nc.vector.tensor_tensor(out=fr[:], in0=th2, in1=n_i[:], op=ALU.subtract)
        fr2 = const.tile([P, 256], F32)
        nc.vector.tensor_tensor(out=fr2[:], in0=fr[:], in1=tl2, op=ALU.add)
        hs = const.tile([P, 256], F32)
        qs = const.tile([P, 256], F32)
        hs2 = const.tile([P, 256], F32)
        qs2 = const.tile([P, 256], F32)

        def tables_scalar():
            nc.scalar.activation(out=hs[:], in_=fr2[:], func=ACT.Sin, scale=PI)
            nc.scalar.activation(out=qs[:], in_=fr2[:], func=ACT.Sin, scale=PI / 2.0)
            nc.scalar.square(out=hs2[:], in_=hs[:])
            nc.scalar.square(out=qs2[:], in_=qs[:])

        ctab = const.tile([P, 4, P], F32)
        stab = const.tile([P, 4, P], F32)

        def tables_vector():
            cpf = const.tile([P, 256], F32)
            nc.vector.tensor_scalar(out=cpf[:], in0=qs2[:], scalar1=-4.0, scalar2=2.0, op0=ALU.mult, op1=ALU.add)
            ctab_v = ctab[:].rearrange("p j (n two) -> p (j n) two", two=2)
            stab_v = stab[:].rearrange("p j (n two) -> p (j n) two", two=2)
            nc.vector.tensor_scalar(
                out=ctab_v, in0=hs2[:].unsqueeze(2).to_broadcast([P, 256, 2]),
                scalar1=-2.0, scalar2=1.0, op0=ALU.mult, op1=ALU.add,
            )
            nc.vector.tensor_tensor(out=stab_v[:, :, 1], in0=hs[:], in1=cpf[:], op=ALU.mult)
            nc.vector.tensor_scalar_mul(out=stab_v[:, :, 0], in0=stab_v[:, :, 1], scalar1=-1.0)

        w_grp = const.tile([P, 2, 384, 4], BF16, align_bytes=64)
        w_grp32 = w_grp[:].bitcast(F32)
        w_raw32 = w_raw[:].bitcast(F32)
        w_codes = const.tile([P, 2, 384], U32, align_bytes=64)
        w_scales = const.tile([P, 2, 384], U8, align_bytes=64)

        def w_transpose(w):
            tp = ps_t.tile([P, 4, P], F32, tag="tp")
            for wb in range(4):
                nc.tensor.transpose(out=tp[:, wb, :], in_=w_raw32[:, w, wb * P:(wb + 1) * P], identity=ident[:])
            state[("wtp", w)] = tp

        def w_copy(w):
            nc.vector.tensor_copy(
                out=w_grp32[:, :, w * P:(w + 1) * P, :],
                in_=state[("wtp", w)][:].rearrange("p (g u) r -> p g r u", u=2),
            )

        def w_quantise(lo, hi):
            for g in range(2):
                nc.vector.quantize_mx(
                    out=w_codes[:, g, lo:hi].bitcast(FP8X4),
                    scales=w_scales[:, g, lo:hi],
                    in_=w_grp[:, g, lo:hi, :].rearrange("p f t -> p (f t)"),
                )

        def transposes(b):
            n, bb = divmod(b, 2)
            x32 = state[("x", n)][:].bitcast(F32)
            grp = gpool.tile([P, 2, 2, P, 4], BF16, tag="grp", align_bytes=64)
            grp32 = grp[:].bitcast(F32)
            for jj in range(2):
                tp = ps_t.tile([P, 4, P], F32, tag="tp")
                for wb in range(4):
                    nc.tensor.transpose(
                        out=tp[:, wb, :], in_=x32[:, 2 * bb + jj, wb * P:(wb + 1) * P], identity=ident[:]
                    )
                nc.scalar.copy(out=grp32[:, jj], in_=tp[:].rearrange("p (g u) r -> p g r u", u=2))
            state[("grp", b)] = grp

        def quantise(b):
            grp = state[("grp", b)]
            codes = kpool.tile([P, 512], U32, tag="codes", align_bytes=64)
            scales = kpool.tile([P, 512], U8, tag="scales", align_bytes=64)
            nc.vector.quantize_mx(
                out=codes[:].bitcast(FP8X4), scales=scales[:],
                in_=grp[:].rearrange("p a g r t -> p (a g r t)"),
            )
            state[("q", b)] = (codes, scales)

        def products(b):
            n, bb = divmod(b, 2)
            codes, scales = state[("q", b)]
            qk = ps_qk.tile([P, 2, 256], F32, tag="qk")
            vb = ps_v.tile([P, 2, P], F32, tag="vb")
            for jj in range(2):
                for g in range(2):
                    c0 = (jj * 2 + g) * P
                    for dst, lo, hi in ((qk[:, jj, :], 0, 256), (vb[:, jj, :], 256, 384)):
                        nc.tensor.matmul_mx(
                            out=dst,
                            lhsT=codes[:, c0:c0 + P].bitcast(FP8X4),
                            lhsT_scale=scales[:, c0:c0 + P],
                            rhs=w_codes[:, g, lo:hi].bitcast(FP8X4),
                            rhs_scale=w_scales[:, g, lo:hi],
                            start=(g == 0), stop=(g == 1),
                        )
            state[("qk", b)] = qk
            if bb == 0:
                yv = ypool.tile([P, 4, P], F32, tag="yv")
                state[("yv", n)] = yv
            nc.scalar.copy(out=state[("yv", n)][:, 2 * bb:2 * bb + 2, :], in_=vb[:])
            if bb == 1:
                nc.sync.dma_start(out=out_v[2][n], in_=state[("yv", n)][:].rearrange("p j f -> p (j f)"))

        def rotate(b):
            n, bb = divmod(b, 2)
            qk = state[("qk", b)]
            shape5 = [P, 2, 2, 64, 2]
            m1 = mpool.tile([P, 512], F32, tag="m1")
            m2 = mpool.tile([P, 512], F32, tag="m2")
            js = slice(2 * bb, 2 * bb + 2)
            ct = ctab[:, js, :].rearrange("p a (n two) -> p a n two", two=2).unsqueeze(2).to_broadcast(shape5)
            st = stab[:, js, :].rearrange("p a (n two) -> p a n two", two=2).unsqueeze(2).to_broadcast(shape5)
            x5 = qk[:].rearrange("p a (q n two) -> p a q n two", q=2, two=2)
            nc.vector.tensor_tensor(
                out=m1[:].rearrange("p (a q n two) -> p a q n two", a=2, q=2, two=2), in0=x5, in1=ct, op=ALU.mult
            )
            nc.vector.tensor_tensor(
                out=m2[:].rearrange("p (a q n two) -> p a q n two", a=2, q=2, two=2),
                in0=x5[:, :, :, :, ::-1], in1=st, op=ALU.mult,
            )
            state[("m", b)] = (m1, m2)

        def finish(b):
            n, bb = divmod(b, 2)
            m1, m2 = state[("m", b)]
            if bb == 0:
                y = ypool.tile([P, 2, 4, P], F32, tag="y")
                state[("y", n)] = y
            y = state[("y", n)]
            js = slice(2 * bb, 2 * bb + 2)
            m1v = m1[:].rearrange("p (a q f) -> p a q f", a=2, q=2)
            m2v = m2[:].rearrange("p (a q f) -> p a q f", a=2, q=2)
            cs = slice(256 * bb, 256 * bb + 256)
            if b == BATCHES - 1:
                for q in range(2):
                    nc.vector.tensor_tensor(out=y[:, q, js, :], in0=m1v[:, :, q, :], in1=m2v[:, :, q, :], op=ALU.add)
                    nc.sync.dma_start(out=out_v[q][n][:, cs], in_=y[:, q, js, :].rearrange("p j f -> p (j f)"))
                return
            nc.gpsimd.tensor_tensor(out=y[:, :, js, :].rearrange("p q a f -> p a q f"), in0=m1v, in1=m2v, op=ALU.add)
            if n == CHUNKS - 1:
                for q in range(2):
                    nc.sync.dma_start(out=out_v[q][n][:, cs], in_=y[:, q, js, :].rearrange("p j f -> p (j f)"))
            elif bb == 1:
                for q in range(2):
                    nc.sync.dma_start(out=out_v[q][n], in_=y[:, q].rearrange("p j f -> p (j f)"))
                if n + AHEAD < CHUNKS:
                    load(n + AHEAD)

        w_transpose(0)
        w_transpose(1)
        w_copy(0)
        w_copy(1)
        tables_scalar()
        transposes(0)
        w_quantise(0, 256)
        w_transpose(2)
        w_copy(2)
        w_quantise(256, 384)
        quantise(0)
        transposes(1)
        tables_vector()
        quantise(1)
        t_done = 1
        q_done = 1
        for k in range(-2, BATCHES, 2):
            for b in (k, k + 1):
                if b >= 0:
                    products(b)
            t_up = min(BATCHES - 1, k + 5) if k >= 0 else 3
            while t_done < t_up:
                t_done += 1
                transposes(t_done)
            for b in (k, k + 1):
                if b >= 0:
                    rotate(b)
                    while q_done < min(BATCHES - 1, b + 3):
                        q_done += 1
                        quantise(q_done)
                    finish(b)
